import numpy as np
import ml_dtypes


def mxq(x, axis, fmt="e4m3"):
    dtype, down = {"e4m3": (ml_dtypes.float8_e4m3fn, 7), "e5m2": (ml_dtypes.float8_e5m2, 14)}[fmt]
    v = np.moveaxis(np.asarray(x, np.float32).astype(ml_dtypes.bfloat16).astype(np.float64), axis, -1)
    blocks = v.reshape(v.shape[:-1] + (-1, 32))
    amax = np.abs(blocks).max(-1, keepdims=True)
    byte = np.maximum(np.where(amax > 0, np.frexp(amax)[1] - 1 + 127, 0) - down, 1)
    scale = np.exp2(byte - 127.0)
    codes = (blocks / scale).astype(np.float32).astype(dtype).astype(np.float64)
    return np.moveaxis((codes * scale).reshape(v.shape), -1, axis)


WIDE = False


def mx_kscale(k):
    if not WIDE:
        return np.ones(k)
    levels = np.array([10, -10, 5, -5, 0])
    a = np.random.permutation(np.resize(levels, k // 512 * 4)).reshape(k // 512, 4)
    idx = np.arange(k)
    return np.exp2(a[idx // 512, idx % 128 // 32])


BF16 = ml_dtypes.bfloat16


def bf(x):
    return np.asarray(x, np.float32).astype(BF16)


def f64(x):
    return np.asarray(x).astype(np.float64)


B, I, H = 1024, 2048, 256


def sigmoid(v):
    return 1.0 / (1.0 + np.exp(-v))


def setup_inputs():
    s = mx_kscale(I)
    return {
        "input_": bf(np.random.standard_normal((B, I)) * s),
        "c_input": bf(np.random.standard_normal((B, 1, H))),
        "h_0": bf(np.random.standard_normal((B, H))),
        "weight_ih": bf(np.random.standard_normal((I, 3 * H)) / np.sqrt(I) / s[:, None]),
        "weight_hh": bf(np.random.standard_normal((H, 3 * H)) / np.sqrt(H)),
        "alpha_weight_ih": bf(np.random.standard_normal((I, H)) / np.sqrt(I) / s[:, None]),
        "alpha_weight_hh": bf(np.random.standard_normal((H, H)) / np.sqrt(H)),
        "bias": bf(np.random.standard_normal(3 * H) * 0.5),
        "alpha_bias": bf(np.random.standard_normal(H) * 0.5),
    }


def reference(input_, c_input, h_0, weight_ih, weight_hh, alpha_weight_ih, alpha_weight_hh, bias, alpha_bias):
    xq = mxq(f64(input_), 1, "e4m3")
    wh_b = f64(h_0) @ f64(weight_hh) + f64(bias)
    wi = xq @ mxq(f64(weight_ih), 0, "e4m3")
    pre = wh_b + wi
    i_gate = sigmoid(pre[:, :H])
    o_gate = sigmoid(pre[:, H:2 * H])
    g = np.tanh(pre[:, 2 * H:])
    c_in = f64(c_input)[:, 0, :]
    alpha = sigmoid((xq @ mxq(f64(alpha_weight_ih), 0, "e4m3")) + f64(alpha_bias) + c_in @ f64(alpha_weight_hh))
    e_i = np.exp(i_gate)
    e_a = np.exp(alpha)
    denom = e_i + e_a
    w_i = e_i / denom
    w_a = e_a / denom
    c_1 = w_i * g + w_a * c_in
    h_1 = o_gate * np.tanh(c_1)
    return (h_1, c_1)

@@ -1,0 +1,246 @@
+from contextlib import ExitStack
+
+import concourse.masks as masks
+import concourse.mybir as mybir
+
+BF16 = mybir.dt.bfloat16
+F32 = mybir.dt.float32
+U32 = mybir.dt.uint32
+U8 = mybir.dt.uint8
+FP8X4 = mybir.dt.float8_e4m3fn_x4
+ACT = mybir.ActivationFunctionType
+ALU = mybir.AluOpType
+
+P = 128
+B = 1024
+K_IN = 2048
+H = 256
+PACK = 4
+K_PASS = P * PACK
+PASSES = K_IN // K_PASS
+ROW_TILES = B // P
+IH_COLS = 3 * H
+GATE_COLS = 4 * H
+BANK = 512
+HALVES = GATE_COLS // BANK
+K_TILES_H = H // P
+
+FLOPS = 2 * B * K_IN * GATE_COLS + 2 * B * H * GATE_COLS
+
+
+def tile_multiinputlstmcell_pa_kernel(
+    tc,
+    input_,
+    c_input,
+    h_0,
+    weight_ih,
+    weight_hh,
+    alpha_weight_ih,
+    alpha_weight_hh,
+    bias,
+    alpha_bias,
+    out_0,
+    out_1,
+):
+    nc = tc.nc
+    with ExitStack() as ctx:
+        const = ctx.enter_context(tc.tile_pool(name="const", bufs=1))
+        x_pool = ctx.enter_context(tc.tile_pool(name="x_pool", bufs=5))
+        stage = ctx.enter_context(tc.tile_pool(name="stage", bufs=2))
+        work = ctx.enter_context(tc.tile_pool(name="work", bufs=2))
+        tp_psum = ctx.enter_context(tc.psum_pool(name="tp_psum", bufs=4))
+        acc_psum = ctx.enter_context(tc.psum_pool(name="acc_psum", bufs=4))
+
+        x_view = input_.rearrange("(p m) k -> p m k", m=ROW_TILES)
+        h1_view = out_0.rearrange("(p m) k -> p m k", m=ROW_TILES)
+        c1_view = out_1.rearrange("(p m) k -> p m k", m=ROW_TILES)
+
+        ident_bf = const.tile([P, P], BF16, name="ident_bf")
+        masks.make_identity(nc, ident_bf[:])
+        ident_f32 = const.tile([P, P], F32, name="ident_f32")
+        masks.make_identity(nc, ident_f32[:])
+        ones = const.tile([P, P], BF16, name="ones")
+        nc.vector.memset(ones[:], 1.0)
+        bias_row = const.tile([P, GATE_COLS], BF16, name="bias_row")
+        nc.vector.memset(bias_row[:], 0.0)
+
+        h_rows = const.tile([P, ROW_TILES, H], BF16, name="h_rows")
+        nc.sync.dma_start(out=h_rows[:], in_=h_0.rearrange("(p m) k -> p m k", m=ROW_TILES))
+        c_rows = const.tile([P, ROW_TILES, H], BF16, name="c_rows")
+        nc.sync.dma_start(
+            out=c_rows[:],
+            in_=c_input.flatten_outer_dims().rearrange("(p m) k -> p m k", m=ROW_TILES),
+        )
+        whh = const.tile([P, K_TILES_H, IH_COLS], BF16, name="whh")
+        nc.sync.dma_start(out=whh[:], in_=weight_hh.rearrange("(kt p) n -> p kt n", p=P))
+        awhh = const.tile([P, K_TILES_H, H], BF16, name="awhh")
+        nc.sync.dma_start(out=awhh[:], in_=alpha_weight_hh.rearrange("(kt p) n -> p kt n", p=P))
+        nc.sync.dma_start(out=bias_row[0:1, 0:IH_COLS], in_=bias.unsqueeze(0))
+        nc.sync.dma_start(out=bias_row[0:1, IH_COLS:GATE_COLS], in_=alpha_bias.unsqueeze(0))
+
+        raw_ih = []
+        raw_al = []
+        for g in range(PASSES):
+            rows = slice(g * K_PASS, (g + 1) * K_PASS)
+            ih = const.tile([P, PACK * IH_COLS], BF16, name="raw_ih%d" % g)
+            nc.sync.dma_start(
+                out=ih[:].rearrange("p (u e c) -> p u e c", u=2, e=2),
+                in_=weight_ih[rows, :].rearrange("(u p e) c -> p u e c", u=2, e=2),
+            )
+            al = const.tile([P, PACK * H], BF16, name="raw_al%d" % g)
+            nc.sync.dma_start(
+                out=al[:].rearrange("p (u e c) -> p u e c", u=2, e=2),
+                in_=alpha_weight_ih[rows, :].rearrange("(u p e) c -> p u e c", u=2, e=2),
+            )
+            raw_ih.append(ih)
+            raw_al.append(al)
+
+        hc_t = const.tile([P, ROW_TILES, 2 * K_TILES_H, P], BF16, name="hc_t")
+        for m in range(ROW_TILES):
+            hc_bank = tp_psum.tile([P, 2 * K_TILES_H, P], BF16, name="hc_bank", tag="tp")
+            for kt in range(K_TILES_H):
+                cols = slice(kt * P, (kt + 1) * P)
+                nc.tensor.transpose(hc_bank[:, kt, :], h_rows[:, m, cols], ident_bf[:])
+                nc.tensor.transpose(hc_bank[:, K_TILES_H + kt, :], c_rows[:, m, cols], ident_bf[:])
+            nc.scalar.copy(out=hc_t[:, m, :, :], in_=hc_bank[:])
+
+        bias_all = const.tile([P, GATE_COLS], F32, name="bias_all")
+        for n in range(HALVES):
+            cols = slice(n * BANK, (n + 1) * BANK)
+            bias_bank = acc_psum.tile([P, BANK], F32, name="bias_bank", tag="acc")
+            nc.tensor.matmul(bias_bank[:], lhsT=ones[:], rhs=bias_row[:, cols], start=True, stop=True)
+            nc.vector.tensor_copy(out=bias_all[:, cols], in_=bias_bank[:])
+
+        w_codes = []
+        w_scales = []
+        for g in range(PASSES):
+            grouped_w = stage.tile([P, GATE_COLS * PACK], BF16, name="grouped_w", align_bytes=64)
+            ih_src = raw_ih[g][:].rearrange("p (t c i) -> p c t i", t=PACK, i=4)
+            al_src = raw_al[g][:].rearrange("p (t c i) -> p c t i", t=PACK, i=4)
+            dst = grouped_w[:].rearrange("p (c i t) -> p c t i", i=4, t=PACK)
+            nc.scalar.copy(out=dst[:, 0 : BANK // 4], in_=ih_src[:, 0 : BANK // 4])
+            nc.scalar.copy(out=dst[:, BANK // 4 : IH_COLS // 4], in_=ih_src[:, BANK // 4 : IH_COLS // 4])
+            nc.vector.tensor_copy(out=dst[:, IH_COLS // 4 : GATE_COLS // 4], in_=al_src)
+            codes = const.tile([P, GATE_COLS], U32, name="w_codes%d" % g, align_bytes=64)
+            scales = const.tile([P, GATE_COLS], U8, name="w_scales%d" % g, align_bytes=64)
+            for n in range(HALVES):
+                cols = slice(n * BANK, (n + 1) * BANK)
+                nc.vector.quantize_mx(
+                    out=codes[:, cols].bitcast(FP8X4),
+                    scales=scales[:, cols],
+                    in_=grouped_w[:, n * BANK * PACK : (n + 1) * BANK * PACK],
+                )
+            w_codes.append(codes)
+            w_scales.append(scales)
+
+        def prepare_x(m):
+            x_rows = x_pool.tile([P, K_IN], BF16, name="x_rows")
+            nc.sync.dma_start(out=x_rows[:], in_=x_view[:, m, :])
+            x_words = x_rows[:].bitcast(F32)
+            grouped_x = stage.tile([P, PASSES * P * PACK], BF16, name="grouped_x", align_bytes=64, bufs=3)
+            grouped_words = grouped_x[:].bitcast(F32).rearrange("p (g r u) -> p g r u", g=PASSES, u=2)
+            for b in range(PASSES // 2):
+                x_bank = tp_psum.tile([P, 4, P], F32, name="x_bank", tag="tp")
+                for j in range(4):
+                    first = (4 * b + j) * P
+                    nc.tensor.transpose(x_bank[:, j, :], x_words[:, first : first + P], ident_f32[:])
+                nc.scalar.copy(
+                    out=grouped_words[:, 2 * b : 2 * b + 2, :, :],
+                    in_=x_bank[:].rearrange("p (g u) r -> p g r u", u=2),
+                )
+            codes = const.tile([P, PASSES * P], U32, name="x_codes%d" % m, align_bytes=64)
+            scales = const.tile([P, PASSES * P], U8, name="x_scales%d" % m, align_bytes=64)
+            nc.vector.quantize_mx(out=codes[:].bitcast(FP8X4), scales=scales[:], in_=grouped_x[:])
+            return codes, scales
+
+        def plain_part(m):
+            plain = const.tile([P, GATE_COLS], F32, name="plain%d" % m)
+            io_bank = acc_psum.tile([P, BANK], F32, name="io_bank", tag="acc")
+            ga_bank = acc_psum.tile([P, BANK], F32, name="ga_bank", tag="acc")
+            for kt in range(K_TILES_H):
+                nc.tensor.matmul(
+                    io_bank[:],
+                    lhsT=hc_t[:, m, kt, :],
+                    rhs=whh[:, kt, 0:BANK],
+                    start=(kt == 0),
+                    stop=(kt == K_TILES_H - 1),
+                )
+            for kt in range(K_TILES_H):
+                nc.tensor.matmul(
+                    ga_bank[:, 0:H],
+                    lhsT=hc_t[:, m, kt, :],
+                    rhs=whh[:, kt, BANK:IH_COLS],
+                    start=(kt == 0),
+                    stop=(kt == K_TILES_H - 1),
+                )
+            for kt in range(K_TILES_H):
+                nc.tensor.matmul(
+                    ga_bank[:, H:BANK],
+                    lhsT=hc_t[:, m, K_TILES_H + kt, :],
+                    rhs=awhh[:, kt, :],
+                    start=(kt == 0),
+                    stop=(kt == K_TILES_H - 1),
+                )
+            nc.vector.tensor_tensor(out=plain[:, 0:BANK], in0=io_bank[:], in1=bias_all[:, 0:BANK], op=ALU.add)
+            nc.vector.tensor_tensor(
+                out=plain[:, BANK:GATE_COLS], in0=ga_bank[:], in1=bias_all[:, BANK:GATE_COLS], op=ALU.add
+            )
+            return plain
+
+        h1_all = const.tile([P, ROW_TILES, H], F32, name="h1_all")
+        c1_all = const.tile([P, ROW_TILES, H], F32, name="c1_all")
+
+        def cell(m, x_codes, x_scales, plain):
+            banks = []
+            for n in range(HALVES):
+                mx_bank = acc_psum.tile([P, BANK], F32, name="mx_bank", tag="acc")
+                banks.append(mx_bank)
+            for g in range(PASSES):
+                for n in range(HALVES):
+                    cols = slice(n * BANK, (n + 1) * BANK)
+                    nc.tensor.matmul_mx(
+                        out=banks[n][:],
+                        lhsT=x_codes[:, g * P : (g + 1) * P].bitcast(FP8X4),
+                        lhsT_scale=x_scales[:, g * P : (g + 1) * P],
+                        rhs=w_codes[g][:, cols].bitcast(FP8X4),
+                        rhs_scale=w_scales[g][:, cols],
+                        start=(g == 0),
+                        stop=(g == PASSES - 1),
+                    )
+            gates = work.tile([P, GATE_COLS], F32, name="gates")
+            for n in range(HALVES):
+                cols = slice(n * BANK, (n + 1) * BANK)
+                nc.vector.tensor_tensor(out=gates[:, cols], in0=banks[n][:], in1=plain[:, cols], op=ALU.add)
+            gate_i = gates[:, 0:H]
+            gate_o = gates[:, H : 2 * H]
+            gate_g = gates[:, 2 * H : 3 * H]
+            gate_a = gates[:, 3 * H : 4 * H]
+            nc.scalar.activation(out=gates[:, 0 : 2 * H], in_=gates[:, 0 : 2 * H], func=ACT.Sigmoid)
+            nc.scalar.activation(out=gate_a, in_=gate_a, func=ACT.Sigmoid)
+            nc.scalar.activation(out=gate_g, in_=gate_g, func=ACT.Tanh)
+            w_i = work.tile([P, H], F32, name="w_i")
+            nc.vector.tensor_tensor(out=w_i[:], in0=gate_i, in1=gate_a, op=ALU.subtract)
+            nc.scalar.activation(out=w_i[:], in_=w_i[:], func=ACT.Sigmoid)
+            mix = work.tile([P, H], F32, name="mix")
+            nc.vector.tensor_tensor(out=mix[:], in0=gate_g, in1=c_rows[:, m, :], op=ALU.subtract)
+            nc.vector.tensor_tensor(out=mix[:], in0=mix[:], in1=w_i[:], op=ALU.mult)
+            nc.vector.tensor_tensor(out=c1_all[:, m, :], in0=mix[:], in1=c_rows[:, m, :], op=ALU.add)
+            tanh_c1 = work.tile([P, H], F32, name="tanh_c1")
+            nc.scalar.activation(out=tanh_c1[:], in_=c1_all[:, m, :], func=ACT.Tanh)
+            nc.vector.tensor_tensor(out=h1_all[:, m, :], in0=gate_o, in1=tanh_c1[:], op=ALU.mult)
+
+        AHEAD = 2
+        quantised = []
+        for m in range(AHEAD):
+            quantised.append(prepare_x(m))
+        plains = []
+        for m in range(ROW_TILES):
+            plains.append(plain_part(m))
+        for m in range(ROW_TILES):
+            if m + AHEAD < ROW_TILES:
+                quantised.append(prepare_x(m + AHEAD))
+            cell(m, quantised[m][0], quantised[m][1], plains[m])
+            if m % 2 == 1:
+                pair = slice(m - 1, m + 1)
+                nc.sync.dma_start(out=c1_view[:, pair, :], in_=c1_all[:, pair, :])
+                nc.sync.dma_start(out=h1_view[:, pair, :], in_=h1_all[:, pair, :])

@@ -222,9 +222,9 @@ def tile_multiinputlstmcell_pa_kernel(
             nc.vector.tensor_tensor(out=w_i[:], in0=gate_i, in1=gate_a, op=ALU.subtract)
             nc.scalar.activation(out=w_i[:], in_=w_i[:], func=ACT.Sigmoid)
             mix = work.tile([P, H], F32, name="mix")
-            nc.vector.tensor_tensor(out=mix[:], in0=gate_g, in1=c_rows[:, m, :], op=ALU.subtract)
-            nc.vector.tensor_tensor(out=mix[:], in0=mix[:], in1=w_i[:], op=ALU.mult)
-            nc.vector.tensor_tensor(out=c1_all[:, m, :], in0=mix[:], in1=c_rows[:, m, :], op=ALU.add)
+            nc.gpsimd.tensor_tensor(out=mix[:], in0=gate_g, in1=c_rows[:, m, :], op=ALU.subtract)
+            nc.gpsimd.tensor_tensor(out=mix[:], in0=mix[:], in1=w_i[:], op=ALU.mult)
+            nc.gpsimd.tensor_tensor(out=c1_all[:, m, :], in0=mix[:], in1=c_rows[:, m, :], op=ALU.add)
             tanh_c1 = work.tile([P, H], F32, name="tanh_c1")
             nc.scalar.activation(out=tanh_c1[:], in_=c1_all[:, m, :], func=ACT.Tanh)
             nc.vector.tensor_tensor(out=h1_all[:, m, :], in0=gate_o, in1=tanh_c1[:], op=ALU.mult)

@@ -24,6 +24,10 @@ GATE_COLS = 4 * H
 BANK = 512
 HALVES = GATE_COLS // BANK
 K_TILES_H = H // P
+RUN = 4
+
+X_AHEAD = 3
+Q_AHEAD = 2
 
 FLOPS = 2 * B * K_IN * GATE_COLS + 2 * B * H * GATE_COLS
 
@@ -46,10 +50,10 @@ def tile_multiinputlstmcell_pa_kernel(
     with ExitStack() as ctx:
         const = ctx.enter_context(tc.tile_pool(name="const", bufs=1))
         x_pool = ctx.enter_context(tc.tile_pool(name="x_pool", bufs=5))
-        stage = ctx.enter_context(tc.tile_pool(name="stage", bufs=2))
-        work = ctx.enter_context(tc.tile_pool(name="work", bufs=2))
-        tp_psum = ctx.enter_context(tc.psum_pool(name="tp_psum", bufs=4))
-        acc_psum = ctx.enter_context(tc.psum_pool(name="acc_psum", bufs=4))
+        stage = ctx.enter_context(tc.tile_pool(name="stage", bufs=3))
+        work = ctx.enter_context(tc.tile_pool(name="work", bufs=3))
+        psum = ctx.enter_context(tc.psum_pool(name="psum", bufs=8))
+        ctx.enter_context(tc.manual_schedule())
 
         x_view = input_.rearrange("(p m) k -> p m k", m=ROW_TILES)
         h1_view = out_0.rearrange("(p m) k -> p m k", m=ROW_TILES)
@@ -75,8 +79,10 @@ def tile_multiinputlstmcell_pa_kernel(
         nc.sync.dma_start(out=whh[:], in_=weight_hh.rearrange("(kt p) n -> p kt n", p=P))
         awhh = const.tile([P, K_TILES_H, H], BF16, name="awhh")
         nc.sync.dma_start(out=awhh[:], in_=alpha_weight_hh.rearrange("(kt p) n -> p kt n", p=P))
-        nc.sync.dma_start(out=bias_row[0:1, 0:IH_COLS], in_=bias.unsqueeze(0))
-        nc.sync.dma_start(out=bias_row[0:1, IH_COLS:GATE_COLS], in_=alpha_bias.unsqueeze(0))
+        bias_2d = bias.unsqueeze(0)
+        nc.sync.dma_start(out=bias_row[0:1, 0:H], in_=bias_2d[:, 0:H])
+        nc.sync.dma_start(out=bias_row[0:1, H:BANK], in_=alpha_bias.unsqueeze(0))
+        nc.sync.dma_start(out=bias_row[0:1, BANK:GATE_COLS], in_=bias_2d[:, H:IH_COLS])
 
         raw_ih = []
         raw_al = []
@@ -95,152 +101,208 @@ def tile_multiinputlstmcell_pa_kernel(
             raw_ih.append(ih)
             raw_al.append(al)
 
-        hc_t = const.tile([P, ROW_TILES, 2 * K_TILES_H, P], BF16, name="hc_t")
+        x_rows = {}
         for m in range(ROW_TILES):
-            hc_bank = tp_psum.tile([P, 2 * K_TILES_H, P], BF16, name="hc_bank", tag="tp")
-            for kt in range(K_TILES_H):
-                cols = slice(kt * P, (kt + 1) * P)
-                nc.tensor.transpose(hc_bank[:, kt, :], h_rows[:, m, cols], ident_bf[:])
-                nc.tensor.transpose(hc_bank[:, K_TILES_H + kt, :], c_rows[:, m, cols], ident_bf[:])
-            nc.scalar.copy(out=hc_t[:, m, :, :], in_=hc_bank[:])
+            x_rows[m] = x_pool.tile([P, K_IN], BF16, name="x_rows")
+            nc.sync.dma_start(out=x_rows[m][:], in_=x_view[:, m, :])
 
-        bias_all = const.tile([P, GATE_COLS], F32, name="bias_all")
-        for n in range(HALVES):
-            cols = slice(n * BANK, (n + 1) * BANK)
-            bias_bank = acc_psum.tile([P, BANK], F32, name="bias_bank", tag="acc")
-            nc.tensor.matmul(bias_bank[:], lhsT=ones[:], rhs=bias_row[:, cols], start=True, stop=True)
-            nc.vector.tensor_copy(out=bias_all[:, cols], in_=bias_bank[:])
-
+        hc_t = const.tile([P, ROW_TILES, 2 * K_TILES_H, P], BF16, name="hc_t")
+        h1_all = const.tile([P, ROW_TILES, H], F32, name="h1_all")
+        c1_all = const.tile([P, ROW_TILES, H], F32, name="c1_all")
         w_codes = []
         w_scales = []
         for g in range(PASSES):
-            grouped_w = stage.tile([P, GATE_COLS * PACK], BF16, name="grouped_w", align_bytes=64)
-            ih_src = raw_ih[g][:].rearrange("p (t c i) -> p c t i", t=PACK, i=4)
-            al_src = raw_al[g][:].rearrange("p (t c i) -> p c t i", t=PACK, i=4)
-            dst = grouped_w[:].rearrange("p (c i t) -> p c t i", i=4, t=PACK)
-            nc.scalar.copy(out=dst[:, 0 : BANK // 4], in_=ih_src[:, 0 : BANK // 4])
-            nc.scalar.copy(out=dst[:, BANK // 4 : IH_COLS // 4], in_=ih_src[:, BANK // 4 : IH_COLS // 4])
-            nc.vector.tensor_copy(out=dst[:, IH_COLS // 4 : GATE_COLS // 4], in_=al_src)
-            codes = const.tile([P, GATE_COLS], U32, name="w_codes%d" % g, align_bytes=64)
-            scales = const.tile([P, GATE_COLS], U8, name="w_scales%d" % g, align_bytes=64)
-            for n in range(HALVES):
-                cols = slice(n * BANK, (n + 1) * BANK)
-                nc.vector.quantize_mx(
-                    out=codes[:, cols].bitcast(FP8X4),
-                    scales=scales[:, cols],
-                    in_=grouped_w[:, n * BANK * PACK : (n + 1) * BANK * PACK],
-                )
-            w_codes.append(codes)
-            w_scales.append(scales)
+            w_codes.append(const.tile([P, GATE_COLS], U32, name="w_codes%d" % g, align_bytes=64))
+            w_scales.append(const.tile([P, GATE_COLS], U8, name="w_scales%d" % g, align_bytes=64))
+        x_codes = []
+        x_scales = []
+        plain = []
+        for m in range(ROW_TILES):
+            x_codes.append(const.tile([P, PASSES * P], U32, name="x_codes%d" % m, align_bytes=64))
+            x_scales.append(const.tile([P, PASSES * P], U8, name="x_scales%d" % m, align_bytes=64))
+            plain.append(const.tile([P, GATE_COLS], F32, name="plain%d" % m))
 
-        def prepare_x(m):
-            x_rows = x_pool.tile([P, K_IN], BF16, name="x_rows")
-            nc.sync.dma_start(out=x_rows[:], in_=x_view[:, m, :])
-            x_words = x_rows[:].bitcast(F32)
-            grouped_x = stage.tile([P, PASSES * P * PACK], BF16, name="grouped_x", align_bytes=64, bufs=3)
-            grouped_words = grouped_x[:].bitcast(F32).rearrange("p (g r u) -> p g r u", g=PASSES, u=2)
-            for b in range(PASSES // 2):
-                x_bank = tp_psum.tile([P, 4, P], F32, name="x_bank", tag="tp")
-                for j in range(4):
-                    first = (4 * b + j) * P
-                    nc.tensor.transpose(x_bank[:, j, :], x_words[:, first : first + P], ident_f32[:])
-                nc.scalar.copy(
-                    out=grouped_words[:, 2 * b : 2 * b + 2, :, :],
-                    in_=x_bank[:].rearrange("p (g u) r -> p g r u", u=2),
-                )
-            codes = const.tile([P, PASSES * P], U32, name="x_codes%d" % m, align_bytes=64)
-            scales = const.tile([P, PASSES * P], U8, name="x_scales%d" % m, align_bytes=64)
-            nc.vector.quantize_mx(out=codes[:].bitcast(FP8X4), scales=scales[:], in_=grouped_x[:])
-            return codes, scales
+        hc_bank = {}
+        plain_bank = {}
+        grouped_w = {}
+        x_bank = {}
+        grouped_x = {}
+        mx_bank = {}
+        gates = {}
+        w_i = {}
+        mix = {}
+        tanh_c1 = {}
 
-        def plain_part(m):
-            plain = const.tile([P, GATE_COLS], F32, name="plain%d" % m)
-            io_bank = acc_psum.tile([P, BANK], F32, name="io_bank", tag="acc")
-            ga_bank = acc_psum.tile([P, BANK], F32, name="ga_bank", tag="acc")
+        def transpose_hc(m):
+            hc_bank[m] = psum.tile([P, 2 * K_TILES_H, P], BF16, name="hc_bank", tag="bank")
+            for kt in range(K_TILES_H):
+                cols = slice(kt * P, (kt + 1) * P)
+                nc.tensor.transpose(hc_bank[m][:, kt, :], h_rows[:, m, cols], ident_bf[:])
+                nc.tensor.transpose(hc_bank[m][:, K_TILES_H + kt, :], c_rows[:, m, cols], ident_bf[:])
+
+        def copy_hc(m):
+            nc.scalar.copy(out=hc_t[:, m, :, :], in_=hc_bank[m][:])
+
+        def plain_matmuls(m):
+            ia = psum.tile([P, BANK], F32, name="ia", tag="bank")
+            og = psum.tile([P, BANK], F32, name="og", tag="bank")
+            plain_bank[m] = [ia, og]
+            last = K_TILES_H - 1
+            nc.tensor.matmul(ia[:, 0:H], lhsT=ones[:], rhs=bias_row[:, 0:H], start=True, stop=False)
             for kt in range(K_TILES_H):
                 nc.tensor.matmul(
-                    io_bank[:],
-                    lhsT=hc_t[:, m, kt, :],
-                    rhs=whh[:, kt, 0:BANK],
-                    start=(kt == 0),
-                    stop=(kt == K_TILES_H - 1),
+                    ia[:, 0:H], lhsT=hc_t[:, m, kt, :], rhs=whh[:, kt, 0:H], start=False, stop=(kt == last)
                 )
+            nc.tensor.matmul(ia[:, H:BANK], lhsT=ones[:], rhs=bias_row[:, H:BANK], start=True, stop=False)
             for kt in range(K_TILES_H):
                 nc.tensor.matmul(
-                    ga_bank[:, 0:H],
-                    lhsT=hc_t[:, m, kt, :],
-                    rhs=whh[:, kt, BANK:IH_COLS],
-                    start=(kt == 0),
-                    stop=(kt == K_TILES_H - 1),
-                )
-            for kt in range(K_TILES_H):
-                nc.tensor.matmul(
-                    ga_bank[:, H:BANK],
+                    ia[:, H:BANK],
                     lhsT=hc_t[:, m, K_TILES_H + kt, :],
                     rhs=awhh[:, kt, :],
-                    start=(kt == 0),
-                    stop=(kt == K_TILES_H - 1),
+                    start=False,
+                    stop=(kt == last),
                 )
-            nc.vector.tensor_tensor(out=plain[:, 0:BANK], in0=io_bank[:], in1=bias_all[:, 0:BANK], op=ALU.add)
-            nc.vector.tensor_tensor(
-                out=plain[:, BANK:GATE_COLS], in0=ga_bank[:], in1=bias_all[:, BANK:GATE_COLS], op=ALU.add
-            )
-            return plain
+            nc.tensor.matmul(og[:], lhsT=ones[:], rhs=bias_row[:, BANK:GATE_COLS], start=True, stop=False)
+            for kt in range(K_TILES_H):
+                nc.tensor.matmul(
+                    og[:], lhsT=hc_t[:, m, kt, :], rhs=whh[:, kt, H:IH_COLS], start=False, stop=(kt == last)
+                )
 
-        h1_all = const.tile([P, ROW_TILES, H], F32, name="h1_all")
-        c1_all = const.tile([P, ROW_TILES, H], F32, name="c1_all")
-
-        def cell(m, x_codes, x_scales, plain):
-            banks = []
+        def copy_plain(m):
             for n in range(HALVES):
-                mx_bank = acc_psum.tile([P, BANK], F32, name="mx_bank", tag="acc")
-                banks.append(mx_bank)
-            for g in range(PASSES):
-                for n in range(HALVES):
-                    cols = slice(n * BANK, (n + 1) * BANK)
+                nc.scalar.copy(out=plain[m][:, n * BANK : (n + 1) * BANK], in_=plain_bank[m][n][:])
+
+        def regroup_w(g, n):
+            grouped_w[g, n] = stage.tile([P, BANK * PACK], BF16, name="grouped_w", align_bytes=64, bufs=4)
+            dst = grouped_w[g, n][:].rearrange("p (c i t) -> p c t i", i=RUN, t=PACK)
+            ih_src = raw_ih[g][:].rearrange("p (t c i) -> p c t i", t=PACK, i=RUN)
+            al_src = raw_al[g][:].rearrange("p (t c i) -> p c t i", t=PACK, i=RUN)
+            if n == 0:
+                nc.vector.tensor_copy(out=dst[:, 0 : H // RUN], in_=ih_src[:, 0 : H // RUN])
+                nc.vector.tensor_copy(out=dst[:, H // RUN : BANK // RUN], in_=al_src)
+            else:
+                nc.vector.tensor_copy(out=dst, in_=ih_src[:, H // RUN : IH_COLS // RUN])
+
+        def quantise_w(g, n):
+            cols = slice(n * BANK, (n + 1) * BANK)
+            nc.vector.quantize_mx(
+                out=w_codes[g][:, cols].bitcast(FP8X4), scales=w_scales[g][:, cols], in_=grouped_w[g, n][:]
+            )
+
+        def transpose_x(m):
+            x_words = x_rows[m][:].bitcast(F32)
+            x_bank[m] = []
+            for b in range(PASSES // 2):
+                bank = psum.tile([P, 4, P], F32, name="x_bank", tag="bank")
+                for j in range(4):
+                    first = (4 * b + j) * P
+                    nc.tensor.transpose(bank[:, j, :], x_words[:, first : first + P], ident_f32[:])
+                x_bank[m].append(bank)
+
+        def copy_x(m):
+            grouped_x[m] = stage.tile([P, PASSES * P * PACK], BF16, name="grouped_x", align_bytes=64)
+            words = grouped_x[m][:].bitcast(F32).rearrange("p (g r u) -> p g r u", g=PASSES, u=2)
+            for b in range(PASSES // 2):
+                nc.scalar.copy(
+                    out=words[:, 2 * b : 2 * b + 2, :, :],
+                    in_=x_bank[m][b][:].rearrange("p (g u) r -> p g r u", u=2),
+                )
+
+        def quantise_x(m):
+            nc.vector.quantize_mx(out=x_codes[m][:].bitcast(FP8X4), scales=x_scales[m][:], in_=grouped_x[m][:])
+
+        def mx_matmuls(m):
+            mx_bank[m] = []
+            for n in range(HALVES):
+                cols = slice(n * BANK, (n + 1) * BANK)
+                bank = psum.tile([P, BANK], F32, name="mx_bank", tag="bank")
+                for g in range(PASSES):
                     nc.tensor.matmul_mx(
-                        out=banks[n][:],
-                        lhsT=x_codes[:, g * P : (g + 1) * P].bitcast(FP8X4),
-                        lhsT_scale=x_scales[:, g * P : (g + 1) * P],
+                        out=bank[:],
+                        lhsT=x_codes[m][:, g * P : (g + 1) * P].bitcast(FP8X4),
+                        lhsT_scale=x_scales[m][:, g * P : (g + 1) * P],
                         rhs=w_codes[g][:, cols].bitcast(FP8X4),
                         rhs_scale=w_scales[g][:, cols],
                         start=(g == 0),
                         stop=(g == PASSES - 1),
                     )
-            gates = work.tile([P, GATE_COLS], F32, name="gates")
+                mx_bank[m].append(bank)
+
+        def add_plain(m):
+            gates[m] = work.tile([P, GATE_COLS], F32, name="gates")
             for n in range(HALVES):
                 cols = slice(n * BANK, (n + 1) * BANK)
-                nc.vector.tensor_tensor(out=gates[:, cols], in0=banks[n][:], in1=plain[:, cols], op=ALU.add)
-            gate_i = gates[:, 0:H]
-            gate_o = gates[:, H : 2 * H]
-            gate_g = gates[:, 2 * H : 3 * H]
-            gate_a = gates[:, 3 * H : 4 * H]
-            nc.scalar.activation(out=gates[:, 0 : 2 * H], in_=gates[:, 0 : 2 * H], func=ACT.Sigmoid)
-            nc.scalar.activation(out=gate_a, in_=gate_a, func=ACT.Sigmoid)
-            nc.scalar.activation(out=gate_g, in_=gate_g, func=ACT.Tanh)
-            w_i = work.tile([P, H], F32, name="w_i")
-            nc.vector.tensor_tensor(out=w_i[:], in0=gate_i, in1=gate_a, op=ALU.subtract)
-            nc.scalar.activation(out=w_i[:], in_=w_i[:], func=ACT.Sigmoid)
-            mix = work.tile([P, H], F32, name="mix")
-            nc.gpsimd.tensor_tensor(out=mix[:], in0=gate_g, in1=c_rows[:, m, :], op=ALU.subtract)
-            nc.gpsimd.tensor_tensor(out=mix[:], in0=mix[:], in1=w_i[:], op=ALU.mult)
-            nc.gpsimd.tensor_tensor(out=c1_all[:, m, :], in0=mix[:], in1=c_rows[:, m, :], op=ALU.add)
-            tanh_c1 = work.tile([P, H], F32, name="tanh_c1")
-            nc.scalar.activation(out=tanh_c1[:], in_=c1_all[:, m, :], func=ACT.Tanh)
-            nc.vector.tensor_tensor(out=h1_all[:, m, :], in0=gate_o, in1=tanh_c1[:], op=ALU.mult)
+                nc.vector.tensor_tensor(out=gates[m][:, cols], in0=mx_bank[m][n][:], in1=plain[m][:, cols], op=ALU.add)
 
-        AHEAD = 2
-        quantised = []
-        for m in range(AHEAD):
-            quantised.append(prepare_x(m))
-        plains = []
-        for m in range(ROW_TILES):
-            plains.append(plain_part(m))
-        for m in range(ROW_TILES):
-            if m + AHEAD < ROW_TILES:
-                quantised.append(prepare_x(m + AHEAD))
-            cell(m, quantised[m][0], quantised[m][1], plains[m])
-            if m % 2 == 1:
-                pair = slice(m - 1, m + 1)
-                nc.sync.dma_start(out=c1_view[:, pair, :], in_=c1_all[:, pair, :])
-                nc.sync.dma_start(out=h1_view[:, pair, :], in_=h1_all[:, pair, :])
+        def activate_gates(m):
+            nc.scalar.activation(out=gates[m][:, 0:BANK], in_=gates[m][:, 0:BANK], func=ACT.Sigmoid)
+            nc.scalar.activation(out=gates[m][:, BANK : BANK + H], in_=gates[m][:, BANK : BANK + H], func=ACT.Sigmoid)
+            nc.scalar.activation(out=gates[m][:, BANK + H :], in_=gates[m][:, BANK + H :], func=ACT.Tanh)
+
+        def gate_difference(m):
+            w_i[m] = work.tile([P, H], F32, name="w_i")
+            nc.vector.tensor_tensor(out=w_i[m][:], in0=gates[m][:, 0:H], in1=gates[m][:, H:BANK], op=ALU.subtract)
+
+        def softmax_weight(m):
+            nc.scalar.activation(out=w_i[m][:], in_=w_i[m][:], func=ACT.Sigmoid)
+
+        def cell_difference(m):
+            mix[m] = work.tile([P, H], F32, name="mix")
+            nc.vector.tensor_tensor(out=mix[m][:], in0=gates[m][:, BANK + H :], in1=c_rows[:, m, :], op=ALU.subtract)
+
+        def new_cell(m):
+            nc.vector.tensor_tensor(out=mix[m][:], in0=mix[m][:], in1=w_i[m][:], op=ALU.mult)
+            nc.vector.tensor_tensor(out=c1_all[:, m, :], in0=mix[m][:], in1=c_rows[:, m, :], op=ALU.add)
+
+        def tanh_cell(m):
+            tanh_c1[m] = work.tile([P, H], F32, name="tanh_c1")
+            nc.scalar.activation(out=tanh_c1[m][:], in_=c1_all[:, m, :], func=ACT.Tanh)
+
+        def new_hidden(m):
+            nc.vector.tensor_tensor(out=h1_all[:, m, :], in0=gates[m][:, BANK : BANK + H], in1=tanh_c1[m][:], op=ALU.mult)
+
+        def store_pair(m):
+            pair = slice(m - 1, m + 1)
+            nc.sync.dma_start(out=c1_view[:, pair, :], in_=c1_all[:, pair, :])
+            nc.sync.dma_start(out=h1_view[:, pair, :], in_=h1_all[:, pair, :])
+
+        for m in range(ROW_TILES + 1):
+            if m < ROW_TILES:
+                transpose_hc(m)
+            if m >= 1:
+                copy_hc(m - 1)
+        plain_matmuls(0)
+        for g in range(PASSES):
+            regroup_w(g, 0)
+            regroup_w(g, 1)
+            for n in range(HALVES):
+                m = HALVES * g + n
+                if m + 1 < ROW_TILES:
+                    plain_matmuls(m + 1)
+                copy_plain(m)
+                quantise_w(g, n)
+
+        for step in range(-X_AHEAD, ROW_TILES + 1):
+            m = step
+            if 0 <= m < ROW_TILES:
+                mx_matmuls(m)
+            if m + X_AHEAD < ROW_TILES:
+                transpose_x(m + X_AHEAD)
+            if 0 <= m < ROW_TILES:
+                add_plain(m)
+                activate_gates(m)
+            if 1 <= m:
+                new_cell(m - 1)
+                tanh_cell(m - 1)
+            if 0 <= m + Q_AHEAD < ROW_TILES:
+                quantise_x(m + Q_AHEAD)
+            if m + X_AHEAD < ROW_TILES:
+                copy_x(m + X_AHEAD)
+            if 0 <= m < ROW_TILES:
+                gate_difference(m)
+                softmax_weight(m)
+                cell_difference(m)
+            if 1 <= m:
+                new_hidden(m - 1)
+                if (m - 1) % 2 == 1:
+                    store_pair(m - 1)

@@ -228,14 +228,16 @@ def tile_multiinputlstmcell_pa_kernel(
                     )
                 mx_bank[m].append(bank)
 
-        def add_plain(m):
-            gates[m] = work.tile([P, GATE_COLS], F32, name="gates")
-            for n in range(HALVES):
-                cols = slice(n * BANK, (n + 1) * BANK)
-                nc.vector.tensor_tensor(out=gates[m][:, cols], in0=mx_bank[m][n][:], in1=plain[m][:, cols], op=ALU.add)
+        def add_plain(m, n):
+            if n == 0:
+                gates[m] = work.tile([P, GATE_COLS], F32, name="gates")
+            cols = slice(n * BANK, (n + 1) * BANK)
+            nc.vector.tensor_tensor(out=gates[m][:, cols], in0=mx_bank[m][n][:], in1=plain[m][:, cols], op=ALU.add)
 
-        def activate_gates(m):
+        def activate_i_alpha(m):
             nc.scalar.activation(out=gates[m][:, 0:BANK], in_=gates[m][:, 0:BANK], func=ACT.Sigmoid)
+
+        def activate_o_g(m):
             nc.scalar.activation(out=gates[m][:, BANK : BANK + H], in_=gates[m][:, BANK : BANK + H], func=ACT.Sigmoid)
             nc.scalar.activation(out=gates[m][:, BANK + H :], in_=gates[m][:, BANK + H :], func=ACT.Tanh)
 
@@ -250,8 +252,10 @@ def tile_multiinputlstmcell_pa_kernel(
             mix[m] = work.tile([P, H], F32, name="mix")
             nc.vector.tensor_tensor(out=mix[m][:], in0=gates[m][:, BANK + H :], in1=c_rows[:, m, :], op=ALU.subtract)
 
-        def new_cell(m):
+        def weigh_difference(m):
             nc.vector.tensor_tensor(out=mix[m][:], in0=mix[m][:], in1=w_i[m][:], op=ALU.mult)
+
+        def new_cell(m):
             nc.vector.tensor_tensor(out=c1_all[:, m, :], in0=mix[m][:], in1=c_rows[:, m, :], op=ALU.add)
 
         def tanh_cell(m):
@@ -261,10 +265,9 @@ def tile_multiinputlstmcell_pa_kernel(
         def new_hidden(m):
             nc.vector.tensor_tensor(out=h1_all[:, m, :], in0=gates[m][:, BANK : BANK + H], in1=tanh_c1[m][:], op=ALU.mult)
 
-        def store_pair(m):
+        def store_pair(view, rows, m):
             pair = slice(m - 1, m + 1)
-            nc.sync.dma_start(out=c1_view[:, pair, :], in_=c1_all[:, pair, :])
-            nc.sync.dma_start(out=h1_view[:, pair, :], in_=h1_all[:, pair, :])
+            nc.sync.dma_start(out=view[:, pair, :], in_=rows[:, pair, :])
 
         for m in range(ROW_TILES + 1):
             if m < ROW_TILES:
@@ -284,25 +287,34 @@ def tile_multiinputlstmcell_pa_kernel(
 
         for step in range(-X_AHEAD, ROW_TILES + 1):
             m = step
-            if 0 <= m < ROW_TILES:
+            now = 0 <= m < ROW_TILES
+            before = 1 <= m
+            if now:
                 mx_matmuls(m)
             if m + X_AHEAD < ROW_TILES:
                 transpose_x(m + X_AHEAD)
-            if 0 <= m < ROW_TILES:
-                add_plain(m)
-                activate_gates(m)
-            if 1 <= m:
+            if now:
+                add_plain(m, 0)
+                activate_i_alpha(m)
+            if before:
+                weigh_difference(m - 1)
+            if now:
+                add_plain(m, 1)
+                activate_o_g(m)
+            if before:
                 new_cell(m - 1)
                 tanh_cell(m - 1)
+                if (m - 1) % 2 == 1:
+                    store_pair(c1_view, c1_all, m - 1)
             if 0 <= m + Q_AHEAD < ROW_TILES:
                 quantise_x(m + Q_AHEAD)
-            if m + X_AHEAD < ROW_TILES:
-                copy_x(m + X_AHEAD)
-            if 0 <= m < ROW_TILES:
+            if now:
                 gate_difference(m)
                 softmax_weight(m)
                 cell_difference(m)
-            if 1 <= m:
+            if m + X_AHEAD < ROW_TILES:
+                copy_x(m + X_AHEAD)
+            if before:
                 new_hidden(m - 1)
                 if (m - 1) % 2 == 1:
-                    store_pair(m - 1)
+                    store_pair(h1_view, h1_all, m - 1)

@@ -250,7 +250,7 @@ def tile_multiinputlstmcell_pa_kernel(
 
         def cell_difference(m):
             mix[m] = work.tile([P, H], F32, name="mix")
-            nc.vector.tensor_tensor(out=mix[m][:], in0=gates[m][:, BANK + H :], in1=c_rows[:, m, :], op=ALU.subtract)
+            nc.gpsimd.tensor_tensor(out=mix[m][:], in0=gates[m][:, BANK + H :], in1=c_rows[:, m, :], op=ALU.subtract)
 
         def weigh_difference(m):
             nc.vector.tensor_tensor(out=mix[m][:], in0=mix[m][:], in1=w_i[m][:], op=ALU.mult)

from contextlib import ExitStack

import concourse.masks as masks
import concourse.mybir as mybir

BF16 = mybir.dt.bfloat16
F32 = mybir.dt.float32
U32 = mybir.dt.uint32
U8 = mybir.dt.uint8
FP8X4 = mybir.dt.float8_e4m3fn_x4
ACT = mybir.ActivationFunctionType
ALU = mybir.AluOpType

P = 128
B = 1024
K_IN = 2048
H = 256
PACK = 4
K_PASS = P * PACK
PASSES = K_IN // K_PASS
ROW_TILES = B // P
IH_COLS = 3 * H
GATE_COLS = 4 * H
BANK = 512
HALVES = GATE_COLS // BANK
K_TILES_H = H // P
RUN = 4

X_AHEAD = 3
Q_AHEAD = 2

FLOPS = 2 * B * K_IN * GATE_COLS + 2 * B * H * GATE_COLS


def tile_multiinputlstmcell_pa_kernel(
    tc,
    input_,
    c_input,
    h_0,
    weight_ih,
    weight_hh,
    alpha_weight_ih,
    alpha_weight_hh,
    bias,
    alpha_bias,
    out_0,
    out_1,
):
    nc = tc.nc
    with ExitStack() as ctx:
        const = ctx.enter_context(tc.tile_pool(name="const", bufs=1))
        x_pool = ctx.enter_context(tc.tile_pool(name="x_pool", bufs=5))
        stage = ctx.enter_context(tc.tile_pool(name="stage", bufs=3))
        work = ctx.enter_context(tc.tile_pool(name="work", bufs=3))
        psum = ctx.enter_context(tc.psum_pool(name="psum", bufs=8))
        ctx.enter_context(tc.manual_schedule())

        x_view = input_.rearrange("(p m) k -> p m k", m=ROW_TILES)
        h1_view = out_0.rearrange("(p m) k -> p m k", m=ROW_TILES)
        c1_view = out_1.rearrange("(p m) k -> p m k", m=ROW_TILES)

        ident_bf = const.tile([P, P], BF16, name="ident_bf")
        masks.make_identity(nc, ident_bf[:])
        ident_f32 = const.tile([P, P], F32, name="ident_f32")
        masks.make_identity(nc, ident_f32[:])
        ones = const.tile([P, P], BF16, name="ones")
        nc.vector.memset(ones[:], 1.0)
        bias_row = const.tile([P, GATE_COLS], BF16, name="bias_row")
        nc.vector.memset(bias_row[:], 0.0)

        h_rows = const.tile([P, ROW_TILES, H], BF16, name="h_rows")
        nc.sync.dma_start(out=h_rows[:], in_=h_0.rearrange("(p m) k -> p m k", m=ROW_TILES))
        c_rows = const.tile([P, ROW_TILES, H], BF16, name="c_rows")
        nc.sync.dma_start(
            out=c_rows[:],
            in_=c_input.flatten_outer_dims().rearrange("(p m) k -> p m k", m=ROW_TILES),
        )
        whh = const.tile([P, K_TILES_H, IH_COLS], BF16, name="whh")
        nc.sync.dma_start(out=whh[:], in_=weight_hh.rearrange("(kt p) n -> p kt n", p=P))
        awhh = const.tile([P, K_TILES_H, H], BF16, name="awhh")
        nc.sync.dma_start(out=awhh[:], in_=alpha_weight_hh.rearrange("(kt p) n -> p kt n", p=P))
        bias_2d = bias.unsqueeze(0)
        nc.sync.dma_start(out=bias_row[0:1, 0:H], in_=bias_2d[:, 0:H])
        nc.sync.dma_start(out=bias_row[0:1, H:BANK], in_=alpha_bias.unsqueeze(0))
        nc.sync.dma_start(out=bias_row[0:1, BANK:GATE_COLS], in_=bias_2d[:, H:IH_COLS])

        raw_ih = []
        raw_al = []
        for g in range(PASSES):
            rows = slice(g * K_PASS, (g + 1) * K_PASS)
            ih = const.tile([P, PACK * IH_COLS], BF16, name="raw_ih%d" % g)
            nc.sync.dma_start(
                out=ih[:].rearrange("p (u e c) -> p u e c", u=2, e=2),
                in_=weight_ih[rows, :].rearrange("(u p e) c -> p u e c", u=2, e=2),
            )
            al = const.tile([P, PACK * H], BF16, name="raw_al%d" % g)
            nc.sync.dma_start(
                out=al[:].rearrange("p (u e c) -> p u e c", u=2, e=2),
                in_=alpha_weight_ih[rows, :].rearrange("(u p e) c -> p u e c", u=2, e=2),
            )
            raw_ih.append(ih)
            raw_al.append(al)

        x_rows = {}
        for m in range(ROW_TILES):
            x_rows[m] = x_pool.tile([P, K_IN], BF16, name="x_rows")
            nc.sync.dma_start(out=x_rows[m][:], in_=x_view[:, m, :])

        hc_t = const.tile([P, ROW_TILES, 2 * K_TILES_H, P], BF16, name="hc_t")
        h1_all = const.tile([P, ROW_TILES, H], F32, name="h1_all")
        c1_all = const.tile([P, ROW_TILES, H], F32, name="c1_all")
        w_codes = []
        w_scales = []
        for g in range(PASSES):
            w_codes.append(const.tile([P, GATE_COLS], U32, name="w_codes%d" % g, align_bytes=64))
            w_scales.append(const.tile([P, GATE_COLS], U8, name="w_scales%d" % g, align_bytes=64))
        x_codes = []
        x_scales = []
        plain = []
        for m in range(ROW_TILES):
            x_codes.append(const.tile([P, PASSES * P], U32, name="x_codes%d" % m, align_bytes=64))
            x_scales.append(const.tile([P, PASSES * P], U8, name="x_scales%d" % m, align_bytes=64))
            plain.append(const.tile([P, GATE_COLS], F32, name="plain%d" % m))

        hc_bank = {}
        plain_bank = {}
        grouped_w = {}
        x_bank = {}
        grouped_x = {}
        mx_bank = {}
        gates = {}
        w_i = {}
        mix = {}
        tanh_c1 = {}

        def transpose_hc(m):
            hc_bank[m] = psum.tile([P, 2 * K_TILES_H, P], BF16, name="hc_bank", tag="bank")
            for kt in range(K_TILES_H):
                cols = slice(kt * P, (kt + 1) * P)
                nc.tensor.transpose(hc_bank[m][:, kt, :], h_rows[:, m, cols], ident_bf[:])
                nc.tensor.transpose(hc_bank[m][:, K_TILES_H + kt, :], c_rows[:, m, cols], ident_bf[:])

        def copy_hc(m):
            nc.scalar.copy(out=hc_t[:, m, :, :], in_=hc_bank[m][:])

        def plain_matmuls(m):
            ia = psum.tile([P, BANK], F32, name="ia", tag="bank")
            og = psum.tile([P, BANK], F32, name="og", tag="bank")
            plain_bank[m] = [ia, og]
            last = K_TILES_H - 1
            nc.tensor.matmul(ia[:, 0:H], lhsT=ones[:], rhs=bias_row[:, 0:H], start=True, stop=False)
            for kt in range(K_TILES_H):
                nc.tensor.matmul(
                    ia[:, 0:H], lhsT=hc_t[:, m, kt, :], rhs=whh[:, kt, 0:H], start=False, stop=(kt == last)
                )
            nc.tensor.matmul(ia[:, H:BANK], lhsT=ones[:], rhs=bias_row[:, H:BANK], start=True, stop=False)
            for kt in range(K_TILES_H):
                nc.tensor.matmul(
                    ia[:, H:BANK],
                    lhsT=hc_t[:, m, K_TILES_H + kt, :],
                    rhs=awhh[:, kt, :],
                    start=False,
                    stop=(kt == last),
                )
            nc.tensor.matmul(og[:], lhsT=ones[:], rhs=bias_row[:, BANK:GATE_COLS], start=True, stop=False)
            for kt in range(K_TILES_H):
                nc.tensor.matmul(
                    og[:], lhsT=hc_t[:, m, kt, :], rhs=whh[:, kt, H:IH_COLS], start=False, stop=(kt == last)
                )

        def copy_plain(m):
            for n in range(HALVES):
                nc.scalar.copy(out=plain[m][:, n * BANK : (n + 1) * BANK], in_=plain_bank[m][n][:])

        def regroup_w(g, n):
            grouped_w[g, n] = stage.tile([P, BANK * PACK], BF16, name="grouped_w", align_bytes=64, bufs=4)
            dst = grouped_w[g, n][:].rearrange("p (c i t) -> p c t i", i=RUN, t=PACK)
            ih_src = raw_ih[g][:].rearrange("p (t c i) -> p c t i", t=PACK, i=RUN)
            al_src = raw_al[g][:].rearrange("p (t c i) -> p c t i", t=PACK, i=RUN)
            if n == 0:
                nc.vector.tensor_copy(out=dst[:, 0 : H // RUN], in_=ih_src[:, 0 : H // RUN])
                nc.vector.tensor_copy(out=dst[:, H // RUN : BANK // RUN], in_=al_src)
            else:
                nc.vector.tensor_copy(out=dst, in_=ih_src[:, H // RUN : IH_COLS // RUN])

        def quantise_w(g, n):
            cols = slice(n * BANK, (n + 1) * BANK)
            nc.vector.quantize_mx(
                out=w_codes[g][:, cols].bitcast(FP8X4), scales=w_scales[g][:, cols], in_=grouped_w[g, n][:]
            )

        def transpose_x(m):
            x_words = x_rows[m][:].bitcast(F32)
            x_bank[m] = []
            for b in range(PASSES // 2):
                bank = psum.tile([P, 4, P], F32, name="x_bank", tag="bank")
                for j in range(4):
                    first = (4 * b + j) * P
                    nc.tensor.transpose(bank[:, j, :], x_words[:, first : first + P], ident_f32[:])
                x_bank[m].append(bank)

        def copy_x(m):
            grouped_x[m] = stage.tile([P, PASSES * P * PACK], BF16, name="grouped_x", align_bytes=64)
            words = grouped_x[m][:].bitcast(F32).rearrange("p (g r u) -> p g r u", g=PASSES, u=2)
            for b in range(PASSES // 2):
                nc.scalar.copy(
                    out=words[:, 2 * b : 2 * b + 2, :, :],
                    in_=x_bank[m][b][:].rearrange("p (g u) r -> p g r u", u=2),
                )

        def quantise_x(m):
            nc.vector.quantize_mx(out=x_codes[m][:].bitcast(FP8X4), scales=x_scales[m][:], in_=grouped_x[m][:])

        def mx_matmuls(m):
            mx_bank[m] = []
            for n in range(HALVES):
                cols = slice(n * BANK, (n + 1) * BANK)
                bank = psum.tile([P, BANK], F32, name="mx_bank", tag="bank")
                for g in range(PASSES):
                    nc.tensor.matmul_mx(
                        out=bank[:],
                        lhsT=x_codes[m][:, g * P : (g + 1) * P].bitcast(FP8X4),
                        lhsT_scale=x_scales[m][:, g * P : (g + 1) * P],
                        rhs=w_codes[g][:, cols].bitcast(FP8X4),
                        rhs_scale=w_scales[g][:, cols],
                        start=(g == 0),
                        stop=(g == PASSES - 1),
                    )
                mx_bank[m].append(bank)

        def add_plain(m, n):
            if n == 0:
                gates[m] = work.tile([P, GATE_COLS], F32, name="gates")
            cols = slice(n * BANK, (n + 1) * BANK)
            nc.vector.tensor_tensor(out=gates[m][:, cols], in0=mx_bank[m][n][:], in1=plain[m][:, cols], op=ALU.add)

        def activate_i_alpha(m):
            nc.scalar.activation(out=gates[m][:, 0:BANK], in_=gates[m][:, 0:BANK], func=ACT.Sigmoid)

        def activate_o_g(m):
            nc.scalar.activation(out=gates[m][:, BANK : BANK + H], in_=gates[m][:, BANK : BANK + H], func=ACT.Sigmoid)
            nc.scalar.activation(out=gates[m][:, BANK + H :], in_=gates[m][:, BANK + H :], func=ACT.Tanh)

        def gate_difference(m):
            w_i[m] = work.tile([P, H], F32, name="w_i")
            nc.vector.tensor_tensor(out=w_i[m][:], in0=gates[m][:, 0:H], in1=gates[m][:, H:BANK], op=ALU.subtract)

        def softmax_weight(m):
            nc.scalar.activation(out=w_i[m][:], in_=w_i[m][:], func=ACT.Sigmoid)

        def cell_difference(m):
            mix[m] = work.tile([P, H], F32, name="mix")
            nc.gpsimd.tensor_tensor(out=mix[m][:], in0=gates[m][:, BANK + H :], in1=c_rows[:, m, :], op=ALU.subtract)

        def weigh_difference(m):
            nc.vector.tensor_tensor(out=mix[m][:], in0=mix[m][:], in1=w_i[m][:], op=ALU.mult)

        def new_cell(m):
            nc.vector.tensor_tensor(out=c1_all[:, m, :], in0=mix[m][:], in1=c_rows[:, m, :], op=ALU.add)

        def tanh_cell(m):
            tanh_c1[m] = work.tile([P, H], F32, name="tanh_c1")
            nc.scalar.activation(out=tanh_c1[m][:], in_=c1_all[:, m, :], func=ACT.Tanh)

        def new_hidden(m):
            nc.vector.tensor_tensor(out=h1_all[:, m, :], in0=gates[m][:, BANK : BANK + H], in1=tanh_c1[m][:], op=ALU.mult)

        def store_pair(view, rows, m):
            pair = slice(m - 1, m + 1)
            nc.sync.dma_start(out=view[:, pair, :], in_=rows[:, pair, :])

        for m in range(ROW_TILES + 1):
            if m < ROW_TILES:
                transpose_hc(m)
            if m >= 1:
                copy_hc(m - 1)
        plain_matmuls(0)
        for g in range(PASSES):
            regroup_w(g, 0)
            regroup_w(g, 1)
            for n in range(HALVES):
                m = HALVES * g + n
                if m + 1 < ROW_TILES:
                    plain_matmuls(m + 1)
                copy_plain(m)
                quantise_w(g, n)

        for step in range(-X_AHEAD, ROW_TILES + 1):
            m = step
            now = 0 <= m < ROW_TILES
            before = 1 <= m
            if now:
                mx_matmuls(m)
            if m + X_AHEAD < ROW_TILES:
                transpose_x(m + X_AHEAD)
            if now:
                add_plain(m, 0)
                activate_i_alpha(m)
            if before:
                weigh_difference(m - 1)
            if now:
                add_plain(m, 1)
                activate_o_g(m)
            if before:
                new_cell(m - 1)
                tanh_cell(m - 1)
                if (m - 1) % 2 == 1:
                    store_pair(c1_view, c1_all, m - 1)
            if 0 <= m + Q_AHEAD < ROW_TILES:
                quantise_x(m + Q_AHEAD)
            if now:
                gate_difference(m)
                softmax_weight(m)
                cell_difference(m)
            if m + X_AHEAD < ROW_TILES:
                copy_x(m + X_AHEAD)
            if before:
                new_hidden(m - 1)
                if (m - 1) % 2 == 1:
                    store_pair(h1_view, h1_all, m - 1)
